import numpy as np
import ml_dtypes


def mxq(x, axis, fmt="e4m3"):
    dtype, down = {"e4m3": (ml_dtypes.float8_e4m3fn, 7), "e5m2": (ml_dtypes.float8_e5m2, 14)}[fmt]
    v = np.moveaxis(np.asarray(x, np.float32).astype(ml_dtypes.bfloat16).astype(np.float64), axis, -1)
    blocks = v.reshape(v.shape[:-1] + (-1, 32))
    amax = np.abs(blocks).max(-1, keepdims=True)
    byte = np.maximum(np.where(amax > 0, np.frexp(amax)[1] - 1 + 127, 0) - down, 1)
    scale = np.exp2(byte - 127.0)
    codes = (blocks / scale).astype(np.float32).astype(dtype).astype(np.float64)
    return np.moveaxis((codes * scale).reshape(v.shape), -1, axis)


WIDE = False


def mx_kscale(k):
    if not WIDE:
        return np.ones(k)
    levels = np.array([10, -10, 5, -5, 0])
    if k % 512:
        return np.exp2(np.random.permutation(np.resize(levels, k // 32))).repeat(32)
    a = np.empty((k // 512, 16))
    for p in range(k // 512):
        a[p, :8] = np.random.permutation(np.resize(levels, 8))
        for g in range(8):
            far = levels[np.abs(levels - a[p, g]) >= 10]
            a[p, g + 8] = far[np.random.randint(len(far))]
    return np.exp2(a.ravel()).repeat(32)


BF16 = ml_dtypes.bfloat16


def bf(x):
    return np.asarray(x, np.float32).astype(BF16)


def f64(x):
    return np.asarray(x).astype(np.float64)


B, N, P, C, HID, NB, E, MAXLEN = 2, 8, 3, 256, 128, 63, 1024, 2056
EPS = 1e-5


def setup_inputs():
    s, t = mx_kscale(E), mx_kscale(E)
    return {"h1": bf(np.maximum(np.random.standard_normal((B, N, N, E)), 0.0) * s),
            "edge_mask": bf(np.random.random((B, N, N)) > 0.15),
            "W2": bf(np.random.standard_normal((E, E)) * 1.4 / np.sqrt(E) / s[:, None] * t),
            "b2": bf(np.random.standard_normal(E) * 0.3 * t),
            "W3": bf(np.random.standard_normal((E, E)) * 1.4 / np.sqrt(E) / t[:, None]),
            "b3": bf(np.random.standard_normal(E) * 0.3),
            "ln_g": bf(1.0 + 0.2 * np.random.standard_normal(E)),
            "ln_b": bf(0.2 * np.random.standard_normal(E))}


def reference(h1, edge_mask, W2, b2, W3, b3, ln_g, ln_b):
    h = np.maximum((mxq(f64(h1), 3, "e4m3") @ mxq(f64(W2), 0, "e4m3")) + f64(b2), 0.0)
    h = (mxq(h, 3, "e4m3") @ mxq(f64(W3), 0, "e4m3")) + f64(b3)
    mu = h.mean(-1, keepdims=True)
    var = h.var(-1, keepdims=True)
    h = (h - mu) / np.sqrt(var + EPS) * f64(ln_g) + f64(ln_b)
    return h * f64(edge_mask)[..., None]

@@ -1,0 +1,264 @@
+import concourse.mybir as mybir
+from concourse.masks import make_identity
+
+F32 = mybir.dt.float32
+BF16 = mybir.dt.bfloat16
+U32 = mybir.dt.uint32
+U8 = mybir.dt.uint8
+FP8X4 = mybir.dt.float8_e4m3fn_x4
+ALU = mybir.AluOpType
+ACT = mybir.ActivationFunctionType
+
+P = 128
+E = 1024
+PACK = 4
+K_PASS = P * PACK
+PASSES = E // K_PASS
+BANK = 512
+HALVES = E // BANK
+BLOCKS = BANK // P
+RUN = 4
+W2_VECTOR_COLS = 288
+W3_VECTOR_COLS = 192
+STORE_COLS = 256
+EPS = 1e-5
+
+FLOPS = 2 * 2 * P * E * E
+
+ROW_B3 = 8
+ROW_G = 16
+ROW_MASK = 24
+ROWS_USED = 32
+
+
+def tile_edgefeaturenet_pb_s_kernel(tc, h1, edge_mask, W2, b2, W3, b3, ln_g, ln_b, out):
+    nc = tc.nc
+    h1_rows = h1.flatten_outer_dims()
+    out_rows = out.flatten_outer_dims()
+    mask_row = edge_mask.rearrange("(o b) i j -> o (b i j)", o=1)
+
+    with (
+        tc.tile_pool(name="keep", bufs=1) as keep,
+        tc.tile_pool(name="stage", bufs=3) as stage,
+        tc.psum_pool(name="psum", bufs=1) as psum,
+        tc.manual_schedule(),
+    ):
+        vecs = keep.tile([P, P], BF16)
+        lnb_row = keep.tile([P, E], BF16)
+        nc.vector.memset(vecs[:], 0.0)
+        nc.vector.memset(lnb_row[:], 0.0)
+        b2_cols = keep.tile([P, HALVES, PACK], BF16)
+        nc.scalar.dma_start(out=b2_cols[:], in_=b2.rearrange("(j p t) -> p j t", p=P, t=PACK))
+        nc.scalar.dma_start(out=vecs[ROW_B3 : ROW_B3 + 8, :], in_=b3.rearrange("(c p) -> c p", p=P))
+        nc.scalar.dma_start(out=vecs[ROW_G : ROW_G + 8, :], in_=ln_g.rearrange("(c p) -> c p", p=P))
+        nc.scalar.dma_start(out=vecs[ROW_MASK : ROW_MASK + 1, :], in_=mask_row)
+
+        w2_raw = keep.tile([P, PASSES, PACK, E], BF16)
+        w3_raw = keep.tile([P, PASSES, PACK, E], BF16)
+        h1_sb = keep.tile([P, E], BF16)
+        w2_view = W2.rearrange("(g p t) n -> p g t n", p=P, t=PACK)
+        w3_view = W3.rearrange("(g p t) n -> p g t n", p=P, t=PACK)
+        pieces = [(g, j) for g in range(PASSES) for j in range(HALVES)]
+        for g, j in pieces:
+            cols = slice(j * BANK, (j + 1) * BANK)
+            nc.sync.dma_start(out=w2_raw[:, g, :, cols], in_=w2_view[:, g, :, cols])
+            if (g, j) == pieces[0]:
+                nc.sync.dma_start(out=h1_sb[:], in_=h1_rows)
+        for g, j in pieces:
+            cols = slice(j * BANK, (j + 1) * BANK)
+            nc.sync.dma_start(out=w3_raw[:, g, :, cols], in_=w3_view[:, g, :, cols])
+        nc.sync.dma_start(out=lnb_row[ROW_MASK : ROW_MASK + 1, :], in_=ln_b.rearrange("(o e) -> o e", o=1))
+
+        ident_f32 = keep.tile([P, P], F32)
+        ident_bf16 = keep.tile([P, P], BF16)
+        make_identity(nc, ident_bf16[:])
+        make_identity(nc, ident_f32[:])
+        eps = keep.tile([P, 1], F32)
+        nc.vector.memset(eps[:], EPS)
+        table_warm = keep.tile([P, 1], F32)
+        nc.scalar.activation(out=table_warm[:], in_=eps[:], func=ACT.Abs_reciprocal_sqrt)
+
+        w2_codes = keep.tile([P, PASSES, E], U32, align_bytes=64)
+        w2_scales = keep.tile([P, PASSES, E], U8, align_bytes=64)
+        w3_codes = keep.tile([P, PASSES, E], U32, align_bytes=64)
+        w3_scales = keep.tile([P, PASSES, E], U8, align_bytes=64)
+        h1_codes = keep.tile([P, PASSES * P], U32, align_bytes=64)
+        h1_scales = keep.tile([P, PASSES * P], U8, align_bytes=64)
+        h_codes = keep.tile([P, PASSES * P], U32, align_bytes=64)
+        h_scales = keep.tile([P, PASSES * P], U8, align_bytes=64)
+
+        def regroup(raw, g, j, vector_cols):
+            grouped = stage.tile([P, BANK, PACK], BF16, align_bytes=64, name="grouped")
+            src = raw[:, g, :, j * BANK : (j + 1) * BANK].rearrange("p t (c i) -> p c t i", i=RUN)
+            if raw is w2_raw:
+                dst = grouped[:].rearrange("p (i c) t -> p c t i", i=RUN)
+            else:
+                dst = grouped[:].rearrange("p (c i) t -> p c t i", i=RUN)
+            cut = vector_cols // RUN
+            nc.vector.tensor_copy(out=dst[:, :cut], in_=src[:, :cut])
+            nc.scalar.copy(out=dst[:, cut:], in_=src[:, cut:])
+            return grouped
+
+        def quantise(grouped, codes, scales, g, j):
+            cols = slice(j * BANK, (j + 1) * BANK)
+            nc.vector.quantize_mx(
+                out=codes[:, g, cols].bitcast(FP8X4),
+                scales=scales[:, g, cols],
+                in_=grouped[:].rearrange("p w t -> p (w t)"),
+            )
+
+        hidden_ps = [psum.tile([P, BLOCKS, P], F32, name="hidden%d" % j) for j in range(HALVES)]
+
+        def layer1(j):
+            for t in range(BLOCKS):
+                units = slice(j * BANK + t * P, j * BANK + (t + 1) * P)
+                for g in range(PASSES):
+                    tokens = slice(g * P, (g + 1) * P)
+                    nc.tensor.matmul_mx(
+                        out=hidden_ps[j][:, t, :],
+                        lhsT=w2_codes[:, g, units].bitcast(FP8X4),
+                        lhsT_scale=w2_scales[:, g, units],
+                        rhs=h1_codes[:, tokens].bitcast(FP8X4),
+                        rhs_scale=h1_scales[:, tokens],
+                        start=(g == 0),
+                        stop=(g == PASSES - 1),
+                    )
+
+        w2_grouped = [regroup(w2_raw, *pieces[0], W2_VECTOR_COLS)]
+
+        vecs_ps = psum.tile([P, P], BF16, tag="vecs_then_y0")
+        nc.tensor.transpose(vecs_ps[:], vecs[:], ident_bf16[:])
+        vecs_t = keep.tile([P, ROWS_USED], BF16)
+        nc.vector.tensor_copy(out=vecs_t[:], in_=vecs_ps[:, :ROWS_USED])
+        mask_col = keep.tile([P, 1], F32)
+        nc.vector.tensor_copy(out=mask_col[:], in_=vecs_ps[:, ROW_MASK : ROW_MASK + 1])
+
+        def spread(row, name):
+            rows_ps = psum.tile([P, E], BF16, name=name)
+            for c in range(E // P):
+                nc.tensor.transpose(
+                    rows_ps[:, c * P : (c + 1) * P],
+                    vecs_t[:, row + c : row + c + 1].to_broadcast([P, P]),
+                    ident_bf16[:],
+                )
+            return rows_ps
+
+        h1_words = h1_sb[:].bitcast(F32).rearrange("r (g p u) -> r g u p", g=PASSES, u=2)
+        h1_ps = psum.tile([P, PASSES * 2, P], F32, tag="h1_then_y1")
+        for g in range(PASSES):
+            for u in range(2):
+                nc.tensor.transpose(h1_ps[:, 2 * g + u, :], h1_words[:, g, u, :], ident_f32[:])
+        h1_grouped = keep.tile([P, PASSES * P * PACK], BF16, align_bytes=64)
+        nc.scalar.copy(
+            out=h1_grouped[:].bitcast(F32).rearrange("p (g r u) -> p g r u", g=PASSES, u=2),
+            in_=h1_ps[:].rearrange("p (g u) r -> p g r u", u=2),
+        )
+
+        w2_grouped.append(regroup(w2_raw, *pieces[1], W2_VECTOR_COLS))
+        quantise(w2_grouped[0], w2_codes, w2_scales, *pieces[0])
+
+        b3_ps = spread(ROW_B3, "b3_ps")
+        b3_all = keep.tile([P, E], BF16)
+        nc.scalar.copy(out=b3_all[:], in_=b3_ps[:])
+
+        for step in range(2, len(pieces)):
+            w2_grouped.append(regroup(w2_raw, *pieces[step], W2_VECTOR_COLS))
+            quantise(w2_grouped[step - 1], w2_codes, w2_scales, *pieces[step - 1])
+        nc.vector.quantize_mx(out=h1_codes[:].bitcast(FP8X4), scales=h1_scales[:], in_=h1_grouped[:])
+        layer1(0)
+
+        w3_grouped = [regroup(w3_raw, *pieces[0], W3_VECTOR_COLS)]
+        quantise(w2_grouped[-1], w2_codes, w2_scales, *pieces[-1])
+        layer1(1)
+
+        g_ps = spread(ROW_G, "g_ps")
+        shift_ps = []
+        for j in range(HALVES):
+            shift_j = psum.tile([P, BANK], F32, name="shift%d" % j)
+            nc.tensor.matmul(
+                shift_j[:], lhsT=vecs[:], rhs=lnb_row[:, j * BANK : (j + 1) * BANK], start=True, stop=True
+            )
+            shift_ps.append(shift_j)
+
+        w3_grouped.append(regroup(w3_raw, *pieces[1], W3_VECTOR_COLS))
+        quantise(w3_grouped[0], w3_codes, w3_scales, *pieces[0])
+        biased = keep.tile([P, HALVES, P, PACK], BF16)
+        for j in range(HALVES):
+            nc.vector.tensor_tensor(
+                out=biased[:, j],
+                in0=hidden_ps[j][:].rearrange("p t r -> p r t"),
+                in1=b2_cols[:, j, :].unsqueeze(1).to_broadcast([P, P, PACK]),
+                op=ALU.add,
+            )
+
+        w3_grouped.append(regroup(w3_raw, *pieces[2], W3_VECTOR_COLS))
+        h_grouped = keep.tile([P, PASSES * P * PACK], BF16, align_bytes=64)
+        nc.vector.tensor_scalar_max(
+            out=h_grouped[:], in0=biased[:].rearrange("p j r t -> p (j r t)"), scalar1=0.0
+        )
+        quantise(w3_grouped[1], w3_codes, w3_scales, *pieces[1])
+        nc.vector.quantize_mx(out=h_codes[:].bitcast(FP8X4), scales=h_scales[:], in_=h_grouped[:])
+
+        y_ps = [
+            psum.tile([P, BANK], F32, name="y0", tag="vecs_then_y0"),
+            psum.tile([P, BANK], F32, name="y1", tag="h1_then_y1"),
+        ]
+
+        def layer2(g, j):
+            tokens = slice(g * P, (g + 1) * P)
+            cols = slice(j * BANK, (j + 1) * BANK)
+            nc.tensor.matmul_mx(
+                out=y_ps[j][:],
+                lhsT=h_codes[:, tokens].bitcast(FP8X4),
+                lhsT_scale=h_scales[:, tokens],
+                rhs=w3_codes[:, g, cols].bitcast(FP8X4),
+                rhs_scale=w3_scales[:, g, cols],
+                start=(g == 0),
+                stop=(g == PASSES - 1),
+            )
+
+        layer2(*pieces[0])
+        layer2(*pieces[1])
+        w3_grouped.append(regroup(w3_raw, *pieces[3], W3_VECTOR_COLS))
+        quantise(w3_grouped[2], w3_codes, w3_scales, *pieces[2])
+        layer2(*pieces[2])
+        quantise(w3_grouped[3], w3_codes, w3_scales, *pieces[3])
+        layer2(*pieces[3])
+
+        z = keep.tile([P, E], F32)
+        stats = keep.tile([P, HALVES, 6], F32)
+        for j in range(HALVES):
+            cols = slice(j * BANK, (j + 1) * BANK)
+            nc.vector.tensor_tensor(out=z[:, cols], in0=y_ps[j][:], in1=b3_all[:, cols], op=ALU.add)
+            nc.vector.bn_stats(out=stats[:, j, :], in_=z[:, cols])
+        mean_var = keep.tile([P, 2], F32)
+        nc.vector.bn_aggr(out=mean_var[:], in_=stats[:].rearrange("p j s -> p (j s)"))
+        rstd = keep.tile([P, 1], F32)
+        nc.scalar.activation(out=rstd[:], in_=mean_var[:, 1:2], func=ACT.Abs_reciprocal_sqrt, bias=eps[:])
+        rstd_mask = keep.tile([P, 1], F32)
+        nc.scalar.activation(out=rstd_mask[:], in_=rstd[:], func=ACT.Copy, scale=mask_col[:])
+        centred = keep.tile([P, E], F32)
+        for j in range(HALVES):
+            cols = slice(j * BANK, (j + 1) * BANK)
+            nc.vector.scalar_tensor_tensor(
+                out=centred[:, cols],
+                in0=z[:, cols],
+                scalar=mean_var[:, 0:1],
+                in1=g_ps[:, cols],
+                op0=ALU.subtract,
+                op1=ALU.mult,
+            )
+        result = keep.tile([P, E], F32)
+        for j in range(HALVES):
+            for s in range(BANK // STORE_COLS):
+                in_bank = slice(s * STORE_COLS, (s + 1) * STORE_COLS)
+                cols = slice(j * BANK + s * STORE_COLS, j * BANK + (s + 1) * STORE_COLS)
+                nc.vector.scalar_tensor_tensor(
+                    out=result[:, cols],
+                    in0=centred[:, cols],
+                    scalar=rstd_mask[:],
+                    in1=shift_ps[j][:, in_bank],
+                    op0=ALU.mult,
+                    op1=ALU.add,
+                )
+                nc.sync.dma_start(out=out_rows[:, cols], in_=result[:, cols])

@@ -53,20 +53,21 @@ def tile_edgefeaturenet_pb_s_kernel(tc, h1, edge_mask, W2, b2, W3, b3, ln_g, ln_
         nc.scalar.dma_start(out=vecs[ROW_G : ROW_G + 8, :], in_=ln_g.rearrange("(c p) -> c p", p=P))
         nc.scalar.dma_start(out=vecs[ROW_MASK : ROW_MASK + 1, :], in_=mask_row)
 
-        w2_raw = keep.tile([P, PASSES, PACK, E], BF16)
-        w3_raw = keep.tile([P, PASSES, PACK, E], BF16)
         h1_sb = keep.tile([P, E], BF16)
         w2_view = W2.rearrange("(g p t) n -> p g t n", p=P, t=PACK)
         w3_view = W3.rearrange("(g p t) n -> p g t n", p=P, t=PACK)
         pieces = [(g, j) for g in range(PASSES) for j in range(HALVES)]
+        w2_raw, w3_raw = {}, {}
         for g, j in pieces:
             cols = slice(j * BANK, (j + 1) * BANK)
-            nc.sync.dma_start(out=w2_raw[:, g, :, cols], in_=w2_view[:, g, :, cols])
+            w2_raw[g, j] = keep.tile([P, PACK, BANK], BF16, name="w2_raw%d%d" % (g, j))
+            nc.sync.dma_start(out=w2_raw[g, j][:], in_=w2_view[:, g, :, cols])
             if (g, j) == pieces[0]:
                 nc.sync.dma_start(out=h1_sb[:], in_=h1_rows)
         for g, j in pieces:
             cols = slice(j * BANK, (j + 1) * BANK)
-            nc.sync.dma_start(out=w3_raw[:, g, :, cols], in_=w3_view[:, g, :, cols])
+            w3_raw[g, j] = keep.tile([P, PACK, BANK], BF16, name="w3_raw%d%d" % (g, j))
+            nc.sync.dma_start(out=w3_raw[g, j][:], in_=w3_view[:, g, :, cols])
         nc.sync.dma_start(out=lnb_row[ROW_MASK : ROW_MASK + 1, :], in_=ln_b.rearrange("(o e) -> o e", o=1))
 
         ident_f32 = keep.tile([P, P], F32)
@@ -89,7 +90,7 @@ def tile_edgefeaturenet_pb_s_kernel(tc, h1, edge_mask, W2, b2, W3, b3, ln_g, ln_
 
         def regroup(raw, g, j, vector_cols):
             grouped = stage.tile([P, BANK, PACK], BF16, align_bytes=64, name="grouped")
-            src = raw[:, g, :, j * BANK : (j + 1) * BANK].rearrange("p t (c i) -> p c t i", i=RUN)
+            src = raw[g, j][:].rearrange("p t (c i) -> p c t i", i=RUN)
             if raw is w2_raw:
                 dst = grouped[:].rearrange("p (i c) t -> p c t i", i=RUN)
             else:

@@ -49,7 +49,6 @@ def tile_edgefeaturenet_pb_s_kernel(tc, h1, edge_mask, W2, b2, W3, b3, ln_g, ln_
         nc.vector.memset(lnb_row[:], 0.0)
         b2_cols = keep.tile([P, HALVES, PACK], BF16)
         nc.scalar.dma_start(out=b2_cols[:], in_=b2.rearrange("(j p t) -> p j t", p=P, t=PACK))
-        nc.scalar.dma_start(out=vecs[ROW_B3 : ROW_B3 + 8, :], in_=b3.rearrange("(c p) -> c p", p=P))
         nc.scalar.dma_start(out=vecs[ROW_G : ROW_G + 8, :], in_=ln_g.rearrange("(c p) -> c p", p=P))
         nc.scalar.dma_start(out=vecs[ROW_MASK : ROW_MASK + 1, :], in_=mask_row)
 
@@ -64,10 +63,13 @@ def tile_edgefeaturenet_pb_s_kernel(tc, h1, edge_mask, W2, b2, W3, b3, ln_g, ln_
             nc.sync.dma_start(out=w2_raw[g, j][:], in_=w2_view[:, g, :, cols])
             if (g, j) == pieces[0]:
                 nc.sync.dma_start(out=h1_sb[:], in_=h1_rows)
-        for g, j in pieces:
+        w3_pieces = [(g, j) for j in range(HALVES) for g in range(PASSES)]
+        for g, j in w3_pieces:
             cols = slice(j * BANK, (j + 1) * BANK)
             w3_raw[g, j] = keep.tile([P, PACK, BANK], BF16, name="w3_raw%d%d" % (g, j))
             nc.sync.dma_start(out=w3_raw[g, j][:], in_=w3_view[:, g, :, cols])
+        b3_all = keep.tile([P, E], BF16)
+        nc.sync.dma_start(out=b3_all[:], in_=b3.partition_broadcast(P))
         nc.sync.dma_start(out=lnb_row[ROW_MASK : ROW_MASK + 1, :], in_=ln_b.rearrange("(o e) -> o e", o=1))
 
         ident_f32 = keep.tile([P, P], F32)
@@ -126,13 +128,7 @@ def tile_edgefeaturenet_pb_s_kernel(tc, h1, edge_mask, W2, b2, W3, b3, ln_g, ln_
                     )
 
         w2_grouped = [regroup(w2_raw, *pieces[0], W2_VECTOR_COLS)]
-
-        vecs_ps = psum.tile([P, P], BF16, tag="vecs_then_y0")
-        nc.tensor.transpose(vecs_ps[:], vecs[:], ident_bf16[:])
-        vecs_t = keep.tile([P, ROWS_USED], BF16)
-        nc.vector.tensor_copy(out=vecs_t[:], in_=vecs_ps[:, :ROWS_USED])
-        mask_col = keep.tile([P, 1], F32)
-        nc.vector.tensor_copy(out=mask_col[:], in_=vecs_ps[:, ROW_MASK : ROW_MASK + 1])
+        quantise(w2_grouped[0], w2_codes, w2_scales, *pieces[0])
 
         def spread(row, name):
             rows_ps = psum.tile([P, E], BF16, name=name)
@@ -156,19 +152,22 @@ def tile_edgefeaturenet_pb_s_kernel(tc, h1, edge_mask, W2, b2, W3, b3, ln_g, ln_
         )
 
         w2_grouped.append(regroup(w2_raw, *pieces[1], W2_VECTOR_COLS))
-        quantise(w2_grouped[0], w2_codes, w2_scales, *pieces[0])
+        nc.vector.quantize_mx(out=h1_codes[:].bitcast(FP8X4), scales=h1_scales[:], in_=h1_grouped[:])
 
-        b3_ps = spread(ROW_B3, "b3_ps")
-        b3_all = keep.tile([P, E], BF16)
-        nc.scalar.copy(out=b3_all[:], in_=b3_ps[:])
+        vecs_ps = psum.tile([P, P], BF16, tag="vecs_then_y0")
+        nc.tensor.transpose(vecs_ps[:], vecs[:], ident_bf16[:])
 
         for step in range(2, len(pieces)):
             w2_grouped.append(regroup(w2_raw, *pieces[step], W2_VECTOR_COLS))
             quantise(w2_grouped[step - 1], w2_codes, w2_scales, *pieces[step - 1])
-        nc.vector.quantize_mx(out=h1_codes[:].bitcast(FP8X4), scales=h1_scales[:], in_=h1_grouped[:])
+            if step == 2:
+                vecs_t = keep.tile([P, ROWS_USED], BF16)
+                nc.vector.tensor_copy(out=vecs_t[:], in_=vecs_ps[:, :ROWS_USED])
+                mask_col = keep.tile([P, 1], F32)
+                nc.vector.tensor_copy(out=mask_col[:], in_=vecs_ps[:, ROW_MASK : ROW_MASK + 1])
         layer1(0)
 
-        w3_grouped = [regroup(w3_raw, *pieces[0], W3_VECTOR_COLS)]
+        w3_grouped = [regroup(w3_raw, *w3_pieces[0], W3_VECTOR_COLS)]
         quantise(w2_grouped[-1], w2_codes, w2_scales, *pieces[-1])
         layer1(1)
 
@@ -181,8 +180,8 @@ def tile_edgefeaturenet_pb_s_kernel(tc, h1, edge_mask, W2, b2, W3, b3, ln_g, ln_
             )
             shift_ps.append(shift_j)
 
-        w3_grouped.append(regroup(w3_raw, *pieces[1], W3_VECTOR_COLS))
-        quantise(w3_grouped[0], w3_codes, w3_scales, *pieces[0])
+        w3_grouped.append(regroup(w3_raw, *w3_pieces[1], W3_VECTOR_COLS))
+        quantise(w3_grouped[0], w3_codes, w3_scales, *w3_pieces[0])
         biased = keep.tile([P, HALVES, P, PACK], BF16)
         for j in range(HALVES):
             nc.vector.tensor_tensor(
@@ -192,12 +191,12 @@ def tile_edgefeaturenet_pb_s_kernel(tc, h1, edge_mask, W2, b2, W3, b3, ln_g, ln_
                 op=ALU.add,
             )
 
-        w3_grouped.append(regroup(w3_raw, *pieces[2], W3_VECTOR_COLS))
+        w3_grouped.append(regroup(w3_raw, *w3_pieces[2], W3_VECTOR_COLS))
         h_grouped = keep.tile([P, PASSES * P * PACK], BF16, align_bytes=64)
         nc.vector.tensor_scalar_max(
             out=h_grouped[:], in0=biased[:].rearrange("p j r t -> p (j r t)"), scalar1=0.0
         )
-        quantise(w3_grouped[1], w3_codes, w3_scales, *pieces[1])
+        quantise(w3_grouped[1], w3_codes, w3_scales, *w3_pieces[1])
         nc.vector.quantize_mx(out=h_codes[:].bitcast(FP8X4), scales=h_scales[:], in_=h_grouped[:])
 
         y_ps = [
@@ -218,24 +217,59 @@ def tile_edgefeaturenet_pb_s_kernel(tc, h1, edge_mask, W2, b2, W3, b3, ln_g, ln_
                 stop=(g == PASSES - 1),
             )
 
-        layer2(*pieces[0])
-        layer2(*pieces[1])
-        w3_grouped.append(regroup(w3_raw, *pieces[3], W3_VECTOR_COLS))
-        quantise(w3_grouped[2], w3_codes, w3_scales, *pieces[2])
-        layer2(*pieces[2])
-        quantise(w3_grouped[3], w3_codes, w3_scales, *pieces[3])
-        layer2(*pieces[3])
-
         z = keep.tile([P, E], F32)
-        stats = keep.tile([P, HALVES, 6], F32)
-        for j in range(HALVES):
-            cols = slice(j * BANK, (j + 1) * BANK)
-            nc.vector.tensor_tensor(out=z[:, cols], in0=y_ps[j][:], in1=b3_all[:, cols], op=ALU.add)
-            nc.vector.bn_stats(out=stats[:, j, :], in_=z[:, cols])
-        mean_var = keep.tile([P, 2], F32)
-        nc.vector.bn_aggr(out=mean_var[:], in_=stats[:].rearrange("p j s -> p (j s)"))
+        first, second = slice(0, BANK), slice(BANK, E)
+
+        layer2(*w3_pieces[0])
+        layer2(*w3_pieces[1])
+        w3_grouped.append(regroup(w3_raw, *w3_pieces[3], W3_VECTOR_COLS))
+        quantise(w3_grouped[2], w3_codes, w3_scales, *w3_pieces[2])
+        layer2(*w3_pieces[2])
+        quantise(w3_grouped[3], w3_codes, w3_scales, *w3_pieces[3])
+        layer2(*w3_pieces[3])
+
+        def add_b3(j, cols, total):
+            nc.vector.scalar_tensor_tensor(
+                out=z[:, cols],
+                in0=y_ps[j][:],
+                scalar=1.0,
+                in1=b3_all[:, cols],
+                op0=ALU.mult,
+                op1=ALU.add,
+                accum_out=total[:],
+            )
+
+        squares = keep.tile([P, E], F32)
+
+        def square(cols, total):
+            nc.scalar.activation(
+                out=squares[:, cols], in_=z[:, cols], func=ACT.Square, bias=neg_m0[:], accum_out=total[:]
+            )
+
+        sum0, sum1 = keep.tile([P, 1], F32, name="sum0"), keep.tile([P, 1], F32, name="sum1")
+        sq0, sq1 = keep.tile([P, 1], F32, name="sq0"), keep.tile([P, 1], F32, name="sq1")
+        add_b3(0, first, sum0)
+        neg_m0 = keep.tile([P, 1], F32)
+        nc.scalar.activation(out=neg_m0[:], in_=sum0[:], func=ACT.Copy, scale=-1.0 / BANK)
+        half_m0 = keep.tile([P, 1], F32)
+        nc.scalar.activation(out=half_m0[:], in_=sum0[:], func=ACT.Copy, scale=1.0 / E)
+        square(first, sq0)
+        var0 = keep.tile([P, 1], F32)
+        nc.scalar.activation(out=var0[:], in_=sq0[:], func=ACT.Identity, scale=1.0 / E, bias=eps[:])
+        add_b3(1, second, sum1)
+        square(second, sq1)
+        mean = keep.tile([P, 1], F32)
+        nc.vector.tensor_scalar(
+            out=mean[:], in0=sum1[:], scalar1=1.0 / E, scalar2=half_m0[:], op0=ALU.mult, op1=ALU.add
+        )
+        shift_sq = keep.tile([P, 1], F32)
+        nc.scalar.activation(out=shift_sq[:], in_=mean[:], func=ACT.Square, bias=neg_m0[:])
+        raw_var = keep.tile([P, 1], F32)
+        nc.scalar.activation(out=raw_var[:], in_=sq1[:], func=ACT.Identity, scale=1.0 / E, bias=var0[:])
         rstd = keep.tile([P, 1], F32)
-        nc.scalar.activation(out=rstd[:], in_=mean_var[:, 1:2], func=ACT.Abs_reciprocal_sqrt, bias=eps[:])
+        nc.scalar.activation(
+            out=rstd[:], in_=shift_sq[:], func=ACT.Abs_reciprocal_sqrt, scale=-1.0, bias=raw_var[:]
+        )
         rstd_mask = keep.tile([P, 1], F32)
         nc.scalar.activation(out=rstd_mask[:], in_=rstd[:], func=ACT.Copy, scale=mask_col[:])
         centred = keep.tile([P, E], F32)
@@ -244,7 +278,7 @@ def tile_edgefeaturenet_pb_s_kernel(tc, h1, edge_mask, W2, b2, W3, b3, ln_g, ln_
             nc.vector.scalar_tensor_tensor(
                 out=centred[:, cols],
                 in0=z[:, cols],
-                scalar=mean_var[:, 0:1],
+                scalar=mean[:],
                 in1=g_ps[:, cols],
                 op0=ALU.subtract,
                 op1=ALU.mult,

@@ -49,6 +49,7 @@ def tile_edgefeaturenet_pb_s_kernel(tc, h1, edge_mask, W2, b2, W3, b3, ln_g, ln_
         nc.vector.memset(lnb_row[:], 0.0)
         b2_cols = keep.tile([P, HALVES, PACK], BF16)
         nc.scalar.dma_start(out=b2_cols[:], in_=b2.rearrange("(j p t) -> p j t", p=P, t=PACK))
+        nc.scalar.dma_start(out=vecs[ROW_B3 : ROW_B3 + 8, :], in_=b3.rearrange("(c p) -> c p", p=P))
         nc.scalar.dma_start(out=vecs[ROW_G : ROW_G + 8, :], in_=ln_g.rearrange("(c p) -> c p", p=P))
         nc.scalar.dma_start(out=vecs[ROW_MASK : ROW_MASK + 1, :], in_=mask_row)
 
@@ -68,8 +69,6 @@ def tile_edgefeaturenet_pb_s_kernel(tc, h1, edge_mask, W2, b2, W3, b3, ln_g, ln_
             cols = slice(j * BANK, (j + 1) * BANK)
             w3_raw[g, j] = keep.tile([P, PACK, BANK], BF16, name="w3_raw%d%d" % (g, j))
             nc.sync.dma_start(out=w3_raw[g, j][:], in_=w3_view[:, g, :, cols])
-        b3_all = keep.tile([P, E], BF16)
-        nc.sync.dma_start(out=b3_all[:], in_=b3.partition_broadcast(P))
         nc.sync.dma_start(out=lnb_row[ROW_MASK : ROW_MASK + 1, :], in_=ln_b.rearrange("(o e) -> o e", o=1))
 
         ident_f32 = keep.tile([P, P], F32)
@@ -165,6 +164,7 @@ def tile_edgefeaturenet_pb_s_kernel(tc, h1, edge_mask, W2, b2, W3, b3, ln_g, ln_
                 nc.vector.tensor_copy(out=vecs_t[:], in_=vecs_ps[:, :ROWS_USED])
                 mask_col = keep.tile([P, 1], F32)
                 nc.vector.tensor_copy(out=mask_col[:], in_=vecs_ps[:, ROW_MASK : ROW_MASK + 1])
+        b3_ps = spread(ROW_B3, "b3_ps")
         layer1(0)
 
         w3_grouped = [regroup(w3_raw, *w3_pieces[0], W3_VECTOR_COLS)]
@@ -223,6 +223,8 @@ def tile_edgefeaturenet_pb_s_kernel(tc, h1, edge_mask, W2, b2, W3, b3, ln_g, ln_
         layer2(*w3_pieces[0])
         layer2(*w3_pieces[1])
         w3_grouped.append(regroup(w3_raw, *w3_pieces[3], W3_VECTOR_COLS))
+        b3_all = keep.tile([P, E], BF16)
+        nc.scalar.copy(out=b3_all[:], in_=b3_ps[:])
         quantise(w3_grouped[2], w3_codes, w3_scales, *w3_pieces[2])
         layer2(*w3_pieces[2])
         quantise(w3_grouped[3], w3_codes, w3_scales, *w3_pieces[3])

@@ -18,6 +18,7 @@ BANK = 512
 HALVES = E // BANK
 BLOCKS = BANK // P
 RUN = 4
+FIRST_VECTOR_COLS = 352
 W2_VECTOR_COLS = 288
 W3_VECTOR_COLS = 192
 STORE_COLS = 256
@@ -25,6 +26,7 @@ EPS = 1e-5
 
 FLOPS = 2 * 2 * P * E * E
 
+ROW_B2 = 0
 ROW_B3 = 8
 ROW_G = 16
 ROW_MASK = 24
@@ -47,8 +49,7 @@ def tile_edgefeaturenet_pb_s_kernel(tc, h1, edge_mask, W2, b2, W3, b3, ln_g, ln_
         lnb_row = keep.tile([P, E], BF16)
         nc.vector.memset(vecs[:], 0.0)
         nc.vector.memset(lnb_row[:], 0.0)
-        b2_cols = keep.tile([P, HALVES, PACK], BF16)
-        nc.scalar.dma_start(out=b2_cols[:], in_=b2.rearrange("(j p t) -> p j t", p=P, t=PACK))
+        nc.scalar.dma_start(out=lnb_row[ROW_B2 : ROW_B2 + 1, :], in_=b2.rearrange("(o e) -> o e", o=1))
         nc.scalar.dma_start(out=vecs[ROW_B3 : ROW_B3 + 8, :], in_=b3.rearrange("(c p) -> c p", p=P))
         nc.scalar.dma_start(out=vecs[ROW_G : ROW_G + 8, :], in_=ln_g.rearrange("(c p) -> c p", p=P))
         nc.scalar.dma_start(out=vecs[ROW_MASK : ROW_MASK + 1, :], in_=mask_row)
@@ -69,7 +70,6 @@ def tile_edgefeaturenet_pb_s_kernel(tc, h1, edge_mask, W2, b2, W3, b3, ln_g, ln_
             cols = slice(j * BANK, (j + 1) * BANK)
             w3_raw[g, j] = keep.tile([P, PACK, BANK], BF16, name="w3_raw%d%d" % (g, j))
             nc.sync.dma_start(out=w3_raw[g, j][:], in_=w3_view[:, g, :, cols])
-        nc.sync.dma_start(out=lnb_row[ROW_MASK : ROW_MASK + 1, :], in_=ln_b.rearrange("(o e) -> o e", o=1))
 
         ident_f32 = keep.tile([P, P], F32)
         ident_bf16 = keep.tile([P, P], BF16)
@@ -126,11 +126,11 @@ def tile_edgefeaturenet_pb_s_kernel(tc, h1, edge_mask, W2, b2, W3, b3, ln_g, ln_
                         stop=(g == PASSES - 1),
                     )
 
-        w2_grouped = [regroup(w2_raw, *pieces[0], W2_VECTOR_COLS)]
+        w2_grouped = [regroup(w2_raw, *pieces[0], FIRST_VECTOR_COLS)]
         quantise(w2_grouped[0], w2_codes, w2_scales, *pieces[0])
 
-        def spread(row, name):
-            rows_ps = psum.tile([P, E], BF16, name=name)
+        def spread(row, name, tag):
+            rows_ps = psum.tile([P, E], BF16, name=name, tag=tag)
             for c in range(E // P):
                 nc.tensor.transpose(
                     rows_ps[:, c * P : (c + 1) * P],
@@ -156,22 +156,34 @@ def tile_edgefeaturenet_pb_s_kernel(tc, h1, edge_mask, W2, b2, W3, b3, ln_g, ln_
         vecs_ps = psum.tile([P, P], BF16, tag="vecs_then_y0")
         nc.tensor.transpose(vecs_ps[:], vecs[:], ident_bf16[:])
 
+        b2_ps = psum.tile([P, HALVES * PACK, P], BF16, tag="b2_then_g")
+        for j in range(HALVES):
+            for t in range(PACK):
+                nc.tensor.transpose(
+                    b2_ps[:, j * PACK + t, :],
+                    lnb_row[:, j * BANK + t : (j + 1) * BANK : PACK],
+                    ident_bf16[:],
+                )
+        nc.sync.dma_start(out=lnb_row[ROW_MASK : ROW_MASK + 1, :], in_=ln_b.rearrange("(o e) -> o e", o=1))
+
         for step in range(2, len(pieces)):
             w2_grouped.append(regroup(w2_raw, *pieces[step], W2_VECTOR_COLS))
             quantise(w2_grouped[step - 1], w2_codes, w2_scales, *pieces[step - 1])
             if step == 2:
+                b2_cols = keep.tile([P, HALVES * PACK], BF16)
+                nc.scalar.copy(out=b2_cols[:], in_=b2_ps[:, :, ROW_B2])
                 vecs_t = keep.tile([P, ROWS_USED], BF16)
                 nc.vector.tensor_copy(out=vecs_t[:], in_=vecs_ps[:, :ROWS_USED])
                 mask_col = keep.tile([P, 1], F32)
-                nc.vector.tensor_copy(out=mask_col[:], in_=vecs_ps[:, ROW_MASK : ROW_MASK + 1])
-        b3_ps = spread(ROW_B3, "b3_ps")
+                nc.gpsimd.tensor_copy(out=mask_col[:], in_=vecs_t[:, ROW_MASK : ROW_MASK + 1])
         layer1(0)
 
         w3_grouped = [regroup(w3_raw, *w3_pieces[0], W3_VECTOR_COLS)]
         quantise(w2_grouped[-1], w2_codes, w2_scales, *pieces[-1])
         layer1(1)
+        b3_ps = spread(ROW_B3, "b3_ps", "b3")
 
-        g_ps = spread(ROW_G, "g_ps")
+        g_ps = spread(ROW_G, "g_ps", "b2_then_g")
         shift_ps = []
         for j in range(HALVES):
             shift_j = psum.tile([P, BANK], F32, name="shift%d" % j)
@@ -187,7 +199,7 @@ def tile_edgefeaturenet_pb_s_kernel(tc, h1, edge_mask, W2, b2, W3, b3, ln_g, ln_
             nc.vector.tensor_tensor(
                 out=biased[:, j],
                 in0=hidden_ps[j][:].rearrange("p t r -> p r t"),
-                in1=b2_cols[:, j, :].unsqueeze(1).to_broadcast([P, P, PACK]),
+                in1=b2_cols[:, j * PACK : (j + 1) * PACK].unsqueeze(1).to_broadcast([P, P, PACK]),
                 op=ALU.add,
             )
 
@@ -256,35 +268,35 @@ def tile_edgefeaturenet_pb_s_kernel(tc, h1, edge_mask, W2, b2, W3, b3, ln_g, ln_
         half_m0 = keep.tile([P, 1], F32)
         nc.scalar.activation(out=half_m0[:], in_=sum0[:], func=ACT.Copy, scale=1.0 / E)
         square(first, sq0)
-        var0 = keep.tile([P, 1], F32)
-        nc.scalar.activation(out=var0[:], in_=sq0[:], func=ACT.Identity, scale=1.0 / E, bias=eps[:])
         add_b3(1, second, sum1)
         square(second, sq1)
+
+        offset = keep.tile([P, 1], F32)
+        nc.gpsimd.tensor_scalar(
+            out=offset[:], in0=sum1[:], scalar1=1.0 / E, scalar2=half_m0[:], op0=ALU.mult, op1=ALU.subtract
+        )
+        var0 = keep.tile([P, 1], F32)
+        nc.gpsimd.tensor_scalar(
+            out=var0[:], in0=sq0[:], scalar1=1.0 / E, scalar2=EPS, op0=ALU.mult, op1=ALU.add
+        )
+        neg_var0 = keep.tile([P, 1], F32)
+        nc.gpsimd.tensor_scalar(
+            out=neg_var0[:], in0=offset[:], scalar1=offset[:], scalar2=var0[:], op0=ALU.mult, op1=ALU.subtract
+        )
+        rstd = keep.tile([P, 1], F32)
+        nc.scalar.activation(
+            out=rstd[:], in_=sq1[:], func=ACT.Abs_reciprocal_sqrt, scale=-1.0 / E, bias=neg_var0[:]
+        )
+        rstd_mask = keep.tile([P, 1], F32)
+        nc.scalar.activation(out=rstd_mask[:], in_=rstd[:], func=ACT.Copy, scale=mask_col[:])
         mean = keep.tile([P, 1], F32)
         nc.vector.tensor_scalar(
             out=mean[:], in0=sum1[:], scalar1=1.0 / E, scalar2=half_m0[:], op0=ALU.mult, op1=ALU.add
         )
-        shift_sq = keep.tile([P, 1], F32)
-        nc.scalar.activation(out=shift_sq[:], in_=mean[:], func=ACT.Square, bias=neg_m0[:])
-        raw_var = keep.tile([P, 1], F32)
-        nc.scalar.activation(out=raw_var[:], in_=sq1[:], func=ACT.Identity, scale=1.0 / E, bias=var0[:])
-        rstd = keep.tile([P, 1], F32)
-        nc.scalar.activation(
-            out=rstd[:], in_=shift_sq[:], func=ACT.Abs_reciprocal_sqrt, scale=-1.0, bias=raw_var[:]
-        )
-        rstd_mask = keep.tile([P, 1], F32)
-        nc.scalar.activation(out=rstd_mask[:], in_=rstd[:], func=ACT.Copy, scale=mask_col[:])
         centred = keep.tile([P, E], F32)
-        for j in range(HALVES):
-            cols = slice(j * BANK, (j + 1) * BANK)
-            nc.vector.scalar_tensor_tensor(
-                out=centred[:, cols],
-                in0=z[:, cols],
-                scalar=mean[:],
-                in1=g_ps[:, cols],
-                op0=ALU.subtract,
-                op1=ALU.mult,
-            )
+        nc.vector.scalar_tensor_tensor(
+            out=centred[:], in0=z[:], scalar=mean[:], in1=g_ps[:], op0=ALU.subtract, op1=ALU.mult
+        )
         result = keep.tile([P, E], F32)
         for j in range(HALVES):
             for s in range(BANK // STORE_COLS):

@@ -48,11 +48,9 @@ def tile_edgefeaturenet_pb_s_kernel(tc, h1, edge_mask, W2, b2, W3, b3, ln_g, ln_
         vecs = keep.tile([P, P], BF16)
         lnb_row = keep.tile([P, E], BF16)
         nc.vector.memset(vecs[:], 0.0)
+        g_row = keep.tile([P, BANK], BF16)
         nc.vector.memset(lnb_row[:], 0.0)
-        nc.scalar.dma_start(out=lnb_row[ROW_B2 : ROW_B2 + 1, :], in_=b2.rearrange("(o e) -> o e", o=1))
-        nc.scalar.dma_start(out=vecs[ROW_B3 : ROW_B3 + 8, :], in_=b3.rearrange("(c p) -> c p", p=P))
-        nc.scalar.dma_start(out=vecs[ROW_G : ROW_G + 8, :], in_=ln_g.rearrange("(c p) -> c p", p=P))
-        nc.scalar.dma_start(out=vecs[ROW_MASK : ROW_MASK + 1, :], in_=mask_row)
+        nc.vector.memset(g_row[:], 0.0)
 
         h1_sb = keep.tile([P, E], BF16)
         w2_view = W2.rearrange("(g p t) n -> p g t n", p=P, t=PACK)
@@ -65,11 +63,17 @@ def tile_edgefeaturenet_pb_s_kernel(tc, h1, edge_mask, W2, b2, W3, b3, ln_g, ln_
             nc.sync.dma_start(out=w2_raw[g, j][:], in_=w2_view[:, g, :, cols])
             if (g, j) == pieces[0]:
                 nc.sync.dma_start(out=h1_sb[:], in_=h1_rows)
+            if (g, j) == pieces[1]:
+                nc.sync.dma_start(out=lnb_row[ROW_B2 : ROW_B2 + 1, :], in_=b2.rearrange("(o e) -> o e", o=1))
         w3_pieces = [(g, j) for j in range(HALVES) for g in range(PASSES)]
         for g, j in w3_pieces:
             cols = slice(j * BANK, (j + 1) * BANK)
             w3_raw[g, j] = keep.tile([P, PACK, BANK], BF16, name="w3_raw%d%d" % (g, j))
             nc.sync.dma_start(out=w3_raw[g, j][:], in_=w3_view[:, g, :, cols])
+            if (g, j) == w3_pieces[0]:
+                nc.sync.dma_start(out=vecs[ROW_B3 : ROW_B3 + 8, :], in_=b3.rearrange("(c p) -> c p", p=P))
+                nc.sync.dma_start(out=vecs[ROW_G : ROW_G + 8, :], in_=ln_g.rearrange("(c p) -> c p", p=P))
+                nc.sync.dma_start(out=vecs[ROW_MASK : ROW_MASK + 1, :], in_=mask_row)
 
         ident_f32 = keep.tile([P, P], F32)
         ident_bf16 = keep.tile([P, P], BF16)
@@ -109,7 +113,7 @@ def tile_edgefeaturenet_pb_s_kernel(tc, h1, edge_mask, W2, b2, W3, b3, ln_g, ln_
                 in_=grouped[:].rearrange("p w t -> p (w t)"),
             )
 
-        hidden_ps = [psum.tile([P, BLOCKS, P], F32, name="hidden%d" % j) for j in range(HALVES)]
+        hidden_ps = [psum.tile([P, BLOCKS, P], F32, name="hidden%d" % j, tag="hidden%d" % j) for j in range(HALVES)]
 
         def layer1(j):
             for t in range(BLOCKS):
@@ -129,9 +133,9 @@ def tile_edgefeaturenet_pb_s_kernel(tc, h1, edge_mask, W2, b2, W3, b3, ln_g, ln_
         w2_grouped = [regroup(w2_raw, *pieces[0], FIRST_VECTOR_COLS)]
         quantise(w2_grouped[0], w2_codes, w2_scales, *pieces[0])
 
-        def spread(row, name, tag):
-            rows_ps = psum.tile([P, E], BF16, name=name, tag=tag)
-            for c in range(E // P):
+        def spread(row, blocks, name, tag):
+            rows_ps = psum.tile([P, blocks * P], BF16, name=name, tag=tag)
+            for c in range(blocks):
                 nc.tensor.transpose(
                     rows_ps[:, c * P : (c + 1) * P],
                     vecs_t[:, row + c : row + c + 1].to_broadcast([P, P]),
@@ -153,9 +157,6 @@ def tile_edgefeaturenet_pb_s_kernel(tc, h1, edge_mask, W2, b2, W3, b3, ln_g, ln_
         w2_grouped.append(regroup(w2_raw, *pieces[1], W2_VECTOR_COLS))
         nc.vector.quantize_mx(out=h1_codes[:].bitcast(FP8X4), scales=h1_scales[:], in_=h1_grouped[:])
 
-        vecs_ps = psum.tile([P, P], BF16, tag="vecs_then_y0")
-        nc.tensor.transpose(vecs_ps[:], vecs[:], ident_bf16[:])
-
         b2_ps = psum.tile([P, HALVES * PACK, P], BF16, tag="b2_then_g")
         for j in range(HALVES):
             for t in range(PACK):
@@ -164,26 +165,33 @@ def tile_edgefeaturenet_pb_s_kernel(tc, h1, edge_mask, W2, b2, W3, b3, ln_g, ln_
                     lnb_row[:, j * BANK + t : (j + 1) * BANK : PACK],
                     ident_bf16[:],
                 )
+        nc.sync.dma_start(
+            out=g_row[ROW_MASK : ROW_MASK + 1, :], in_=ln_g.rearrange("(j o n) -> j o n", j=HALVES, o=1)[0]
+        )
         nc.sync.dma_start(out=lnb_row[ROW_MASK : ROW_MASK + 1, :], in_=ln_b.rearrange("(o e) -> o e", o=1))
 
         for step in range(2, len(pieces)):
             w2_grouped.append(regroup(w2_raw, *pieces[step], W2_VECTOR_COLS))
             quantise(w2_grouped[step - 1], w2_codes, w2_scales, *pieces[step - 1])
-            if step == 2:
-                b2_cols = keep.tile([P, HALVES * PACK], BF16)
-                nc.scalar.copy(out=b2_cols[:], in_=b2_ps[:, :, ROW_B2])
-                vecs_t = keep.tile([P, ROWS_USED], BF16)
-                nc.vector.tensor_copy(out=vecs_t[:], in_=vecs_ps[:, :ROWS_USED])
-                mask_col = keep.tile([P, 1], F32)
-                nc.gpsimd.tensor_copy(out=mask_col[:], in_=vecs_t[:, ROW_MASK : ROW_MASK + 1])
         layer1(0)
 
         w3_grouped = [regroup(w3_raw, *w3_pieces[0], W3_VECTOR_COLS)]
+        b2_cols = keep.tile([P, HALVES * PACK], BF16)
+        nc.scalar.copy(out=b2_cols[:], in_=b2_ps[:, :, ROW_B2])
         quantise(w2_grouped[-1], w2_codes, w2_scales, *pieces[-1])
+        vecs_ps = psum.tile([P, P], BF16, tag="vecs_then_y0")
+        nc.tensor.transpose(vecs_ps[:], vecs[:], ident_bf16[:])
         layer1(1)
-        b3_ps = spread(ROW_B3, "b3_ps", "b3")
 
-        g_ps = spread(ROW_G, "g_ps", "b2_then_g")
+        w3_grouped.append(regroup(w3_raw, *w3_pieces[1], W3_VECTOR_COLS))
+        quantise(w3_grouped[0], w3_codes, w3_scales, *w3_pieces[0])
+        vecs_t = keep.tile([P, ROWS_USED], BF16)
+        nc.vector.tensor_copy(out=vecs_t[:], in_=vecs_ps[:, :ROWS_USED])
+        mask_col = keep.tile([P, 1], F32)
+        nc.gpsimd.tensor_copy(out=mask_col[:], in_=vecs_t[:, ROW_MASK : ROW_MASK + 1])
+        b3_ps = spread(ROW_B3, E // P, "b3_ps", "b3")
+
+        g1_ps = spread(ROW_G + BLOCKS, BLOCKS, "g1_ps", "b2_then_g")
         shift_ps = []
         for j in range(HALVES):
             shift_j = psum.tile([P, BANK], F32, name="shift%d" % j)
@@ -192,8 +200,6 @@ def tile_edgefeaturenet_pb_s_kernel(tc, h1, edge_mask, W2, b2, W3, b3, ln_g, ln_
             )
             shift_ps.append(shift_j)
 
-        w3_grouped.append(regroup(w3_raw, *w3_pieces[1], W3_VECTOR_COLS))
-        quantise(w3_grouped[0], w3_codes, w3_scales, *w3_pieces[0])
         biased = keep.tile([P, HALVES, P, PACK], BF16)
         for j in range(HALVES):
             nc.vector.tensor_tensor(
@@ -210,6 +216,9 @@ def tile_edgefeaturenet_pb_s_kernel(tc, h1, edge_mask, W2, b2, W3, b3, ln_g, ln_
         )
         quantise(w3_grouped[1], w3_codes, w3_scales, *w3_pieces[1])
         nc.vector.quantize_mx(out=h_codes[:].bitcast(FP8X4), scales=h_scales[:], in_=h_grouped[:])
+
+        g0_ps = psum.tile([P, BANK], F32, name="g0_ps", tag="hidden0")
+        nc.tensor.matmul(g0_ps[:], lhsT=vecs[:], rhs=g_row[:], start=True, stop=True)
 
         y_ps = [
             psum.tile([P, BANK], F32, name="y0", tag="vecs_then_y0"),
@@ -294,9 +303,10 @@ def tile_edgefeaturenet_pb_s_kernel(tc, h1, edge_mask, W2, b2, W3, b3, ln_g, ln_
             out=mean[:], in0=sum1[:], scalar1=1.0 / E, scalar2=half_m0[:], op0=ALU.mult, op1=ALU.add
         )
         centred = keep.tile([P, E], F32)
-        nc.vector.scalar_tensor_tensor(
-            out=centred[:], in0=z[:], scalar=mean[:], in1=g_ps[:], op0=ALU.subtract, op1=ALU.mult
-        )
+        for cols, gain in ((first, g0_ps), (second, g1_ps)):
+            nc.vector.scalar_tensor_tensor(
+                out=centred[:, cols], in0=z[:, cols], scalar=mean[:], in1=gain[:], op0=ALU.subtract, op1=ALU.mult
+            )
         result = keep.tile([P, E], F32)
         for j in range(HALVES):
             for s in range(BANK // STORE_COLS):
@@ -305,7 +315,7 @@ def tile_edgefeaturenet_pb_s_kernel(tc, h1, edge_mask, W2, b2, W3, b3, ln_g, ln_
                 nc.vector.scalar_tensor_tensor(
                     out=result[:, cols],
                     in0=centred[:, cols],
-                    scalar=rstd_mask[:],
+                    scalar=(rstd if j == 0 else rstd_mask)[:],
                     in1=shift_ps[j][:, in_bank],
                     op0=ALU.mult,
                     op1=ALU.add,

@@ -191,15 +191,6 @@ def tile_edgefeaturenet_pb_s_kernel(tc, h1, edge_mask, W2, b2, W3, b3, ln_g, ln_
         nc.gpsimd.tensor_copy(out=mask_col[:], in_=vecs_t[:, ROW_MASK : ROW_MASK + 1])
         b3_ps = spread(ROW_B3, E // P, "b3_ps", "b3")
 
-        g1_ps = spread(ROW_G + BLOCKS, BLOCKS, "g1_ps", "b2_then_g")
-        shift_ps = []
-        for j in range(HALVES):
-            shift_j = psum.tile([P, BANK], F32, name="shift%d" % j)
-            nc.tensor.matmul(
-                shift_j[:], lhsT=vecs[:], rhs=lnb_row[:, j * BANK : (j + 1) * BANK], start=True, stop=True
-            )
-            shift_ps.append(shift_j)
-
         biased = keep.tile([P, HALVES, P, PACK], BF16)
         for j in range(HALVES):
             nc.vector.tensor_tensor(
@@ -216,9 +207,6 @@ def tile_edgefeaturenet_pb_s_kernel(tc, h1, edge_mask, W2, b2, W3, b3, ln_g, ln_
         )
         quantise(w3_grouped[1], w3_codes, w3_scales, *w3_pieces[1])
         nc.vector.quantize_mx(out=h_codes[:].bitcast(FP8X4), scales=h_scales[:], in_=h_grouped[:])
-
-        g0_ps = psum.tile([P, BANK], F32, name="g0_ps", tag="hidden0")
-        nc.tensor.matmul(g0_ps[:], lhsT=vecs[:], rhs=g_row[:], start=True, stop=True)
 
         y_ps = [
             psum.tile([P, BANK], F32, name="y0", tag="vecs_then_y0"),
@@ -250,6 +238,17 @@ def tile_edgefeaturenet_pb_s_kernel(tc, h1, edge_mask, W2, b2, W3, b3, ln_g, ln_
         layer2(*w3_pieces[2])
         quantise(w3_grouped[3], w3_codes, w3_scales, *w3_pieces[3])
         layer2(*w3_pieces[3])
+
+        g0_ps = psum.tile([P, BANK], F32, name="g0_ps", tag="hidden0")
+        nc.tensor.matmul(g0_ps[:], lhsT=vecs[:], rhs=g_row[:], start=True, stop=True)
+        g1_ps = spread(ROW_G + BLOCKS, BLOCKS, "g1_ps", "b2_then_g")
+        shift_ps = []
+        for j in range(HALVES):
+            shift_j = psum.tile([P, BANK], F32, name="shift%d" % j)
+            nc.tensor.matmul(
+                shift_j[:], lhsT=vecs[:], rhs=lnb_row[:, j * BANK : (j + 1) * BANK], start=True, stop=True
+            )
+            shift_ps.append(shift_j)
 
         def add_b3(j, cols, total):
             nc.vector.scalar_tensor_tensor(

@@ -21,7 +21,7 @@ RUN = 4
 FIRST_VECTOR_COLS = 352
 W2_VECTOR_COLS = 288
 W3_VECTOR_COLS = 192
-STORE_COLS = 256
+STORE_CUTS = (256, 320)
 EPS = 1e-5
 
 FLOPS = 2 * 2 * P * E * E
@@ -46,9 +46,13 @@ def tile_edgefeaturenet_pb_s_kernel(tc, h1, edge_mask, W2, b2, W3, b3, ln_g, ln_
         tc.manual_schedule(),
     ):
         vecs = keep.tile([P, P], BF16)
+        b2_row = keep.tile([P, E], BF16)
         lnb_row = keep.tile([P, E], BF16)
-        nc.vector.memset(vecs[:], 0.0)
         g_row = keep.tile([P, BANK], BF16)
+        one = keep.tile([P, 1], F32)
+        nc.vector.memset(one[:], 1.0)
+        nc.vector.memset(b2_row[:], 0.0)
+        nc.vector.memset(vecs[:], 0.0)
         nc.vector.memset(lnb_row[:], 0.0)
         nc.vector.memset(g_row[:], 0.0)
 
@@ -64,7 +68,7 @@ def tile_edgefeaturenet_pb_s_kernel(tc, h1, edge_mask, W2, b2, W3, b3, ln_g, ln_
             if (g, j) == pieces[0]:
                 nc.sync.dma_start(out=h1_sb[:], in_=h1_rows)
             if (g, j) == pieces[1]:
-                nc.sync.dma_start(out=lnb_row[ROW_B2 : ROW_B2 + 1, :], in_=b2.rearrange("(o e) -> o e", o=1))
+                nc.sync.dma_start(out=b2_row[ROW_B2 : ROW_B2 + 1, :], in_=b2.rearrange("(o e) -> o e", o=1))
         w3_pieces = [(g, j) for j in range(HALVES) for g in range(PASSES)]
         for g, j in w3_pieces:
             cols = slice(j * BANK, (j + 1) * BANK)
@@ -74,15 +78,14 @@ def tile_edgefeaturenet_pb_s_kernel(tc, h1, edge_mask, W2, b2, W3, b3, ln_g, ln_
                 nc.sync.dma_start(out=vecs[ROW_B3 : ROW_B3 + 8, :], in_=b3.rearrange("(c p) -> c p", p=P))
                 nc.sync.dma_start(out=vecs[ROW_G : ROW_G + 8, :], in_=ln_g.rearrange("(c p) -> c p", p=P))
                 nc.sync.dma_start(out=vecs[ROW_MASK : ROW_MASK + 1, :], in_=mask_row)
+                nc.sync.dma_start(out=lnb_row[ROW_MASK : ROW_MASK + 1, :], in_=ln_b.rearrange("(o e) -> o e", o=1))
 
         ident_f32 = keep.tile([P, P], F32)
         ident_bf16 = keep.tile([P, P], BF16)
         make_identity(nc, ident_bf16[:])
         make_identity(nc, ident_f32[:])
-        eps = keep.tile([P, 1], F32)
-        nc.vector.memset(eps[:], EPS)
         table_warm = keep.tile([P, 1], F32)
-        nc.scalar.activation(out=table_warm[:], in_=eps[:], func=ACT.Abs_reciprocal_sqrt)
+        nc.scalar.activation(out=table_warm[:], in_=one[:], func=ACT.Abs_reciprocal_sqrt)
 
         w2_codes = keep.tile([P, PASSES, E], U32, align_bytes=64)
         w2_scales = keep.tile([P, PASSES, E], U8, align_bytes=64)
@@ -162,13 +165,12 @@ def tile_edgefeaturenet_pb_s_kernel(tc, h1, edge_mask, W2, b2, W3, b3, ln_g, ln_
             for t in range(PACK):
                 nc.tensor.transpose(
                     b2_ps[:, j * PACK + t, :],
-                    lnb_row[:, j * BANK + t : (j + 1) * BANK : PACK],
+                    b2_row[:, j * BANK + t : (j + 1) * BANK : PACK],
                     ident_bf16[:],
                 )
         nc.sync.dma_start(
             out=g_row[ROW_MASK : ROW_MASK + 1, :], in_=ln_g.rearrange("(j o n) -> j o n", j=HALVES, o=1)[0]
         )
-        nc.sync.dma_start(out=lnb_row[ROW_MASK : ROW_MASK + 1, :], in_=ln_b.rearrange("(o e) -> o e", o=1))
 
         for step in range(2, len(pieces)):
             w2_grouped.append(regroup(w2_raw, *pieces[step], W2_VECTOR_COLS))
@@ -190,6 +192,13 @@ def tile_edgefeaturenet_pb_s_kernel(tc, h1, edge_mask, W2, b2, W3, b3, ln_g, ln_
         mask_col = keep.tile([P, 1], F32)
         nc.gpsimd.tensor_copy(out=mask_col[:], in_=vecs_t[:, ROW_MASK : ROW_MASK + 1])
         b3_ps = spread(ROW_B3, E // P, "b3_ps", "b3")
+        shift_ps = []
+        for j in range(HALVES):
+            shift_j = psum.tile([P, BANK], F32, name="shift%d" % j)
+            nc.tensor.matmul(
+                shift_j[:], lhsT=vecs[:], rhs=lnb_row[:, j * BANK : (j + 1) * BANK], start=True, stop=True
+            )
+            shift_ps.append(shift_j)
 
         biased = keep.tile([P, HALVES, P, PACK], BF16)
         for j in range(HALVES):
@@ -242,13 +251,6 @@ def tile_edgefeaturenet_pb_s_kernel(tc, h1, edge_mask, W2, b2, W3, b3, ln_g, ln_
         g0_ps = psum.tile([P, BANK], F32, name="g0_ps", tag="hidden0")
         nc.tensor.matmul(g0_ps[:], lhsT=vecs[:], rhs=g_row[:], start=True, stop=True)
         g1_ps = spread(ROW_G + BLOCKS, BLOCKS, "g1_ps", "b2_then_g")
-        shift_ps = []
-        for j in range(HALVES):
-            shift_j = psum.tile([P, BANK], F32, name="shift%d" % j)
-            nc.tensor.matmul(
-                shift_j[:], lhsT=vecs[:], rhs=lnb_row[:, j * BANK : (j + 1) * BANK], start=True, stop=True
-            )
-            shift_ps.append(shift_j)
 
         def add_b3(j, cols, total):
             nc.vector.scalar_tensor_tensor(
@@ -308,9 +310,9 @@ def tile_edgefeaturenet_pb_s_kernel(tc, h1, edge_mask, W2, b2, W3, b3, ln_g, ln_
             )
         result = keep.tile([P, E], F32)
         for j in range(HALVES):
-            for s in range(BANK // STORE_COLS):
-                in_bank = slice(s * STORE_COLS, (s + 1) * STORE_COLS)
-                cols = slice(j * BANK + s * STORE_COLS, j * BANK + (s + 1) * STORE_COLS)
+            for lo, hi in ((0, STORE_CUTS[j]), (STORE_CUTS[j], BANK)):
+                in_bank = slice(lo, hi)
+                cols = slice(j * BANK + lo, j * BANK + hi)
                 nc.vector.scalar_tensor_tensor(
                     out=result[:, cols],
                     in0=centred[:, cols],

import concourse.mybir as mybir
from concourse.masks import make_identity

F32 = mybir.dt.float32
BF16 = mybir.dt.bfloat16
U32 = mybir.dt.uint32
U8 = mybir.dt.uint8
FP8X4 = mybir.dt.float8_e4m3fn_x4
ALU = mybir.AluOpType
ACT = mybir.ActivationFunctionType

P = 128
E = 1024
PACK = 4
K_PASS = P * PACK
PASSES = E // K_PASS
BANK = 512
HALVES = E // BANK
BLOCKS = BANK // P
RUN = 4
FIRST_VECTOR_COLS = 352
W2_VECTOR_COLS = 288
W3_VECTOR_COLS = 192
STORE_CUTS = (256, 320)
EPS = 1e-5

FLOPS = 2 * 2 * P * E * E

ROW_B2 = 0
ROW_B3 = 8
ROW_G = 16
ROW_MASK = 24
ROWS_USED = 32


def tile_edgefeaturenet_pb_s_kernel(tc, h1, edge_mask, W2, b2, W3, b3, ln_g, ln_b, out):
    nc = tc.nc
    h1_rows = h1.flatten_outer_dims()
    out_rows = out.flatten_outer_dims()
    mask_row = edge_mask.rearrange("(o b) i j -> o (b i j)", o=1)

    with (
        tc.tile_pool(name="keep", bufs=1) as keep,
        tc.tile_pool(name="stage", bufs=3) as stage,
        tc.psum_pool(name="psum", bufs=1) as psum,
        tc.manual_schedule(),
    ):
        vecs = keep.tile([P, P], BF16)
        b2_row = keep.tile([P, E], BF16)
        lnb_row = keep.tile([P, E], BF16)
        g_row = keep.tile([P, BANK], BF16)
        one = keep.tile([P, 1], F32)
        nc.vector.memset(one[:], 1.0)
        nc.vector.memset(b2_row[:], 0.0)
        nc.vector.memset(vecs[:], 0.0)
        nc.vector.memset(lnb_row[:], 0.0)
        nc.vector.memset(g_row[:], 0.0)

        h1_sb = keep.tile([P, E], BF16)
        w2_view = W2.rearrange("(g p t) n -> p g t n", p=P, t=PACK)
        w3_view = W3.rearrange("(g p t) n -> p g t n", p=P, t=PACK)
        pieces = [(g, j) for g in range(PASSES) for j in range(HALVES)]
        w2_raw, w3_raw = {}, {}
        for g, j in pieces:
            cols = slice(j * BANK, (j + 1) * BANK)
            w2_raw[g, j] = keep.tile([P, PACK, BANK], BF16, name="w2_raw%d%d" % (g, j))
            nc.sync.dma_start(out=w2_raw[g, j][:], in_=w2_view[:, g, :, cols])
            if (g, j) == pieces[0]:
                nc.sync.dma_start(out=h1_sb[:], in_=h1_rows)
            if (g, j) == pieces[1]:
                nc.sync.dma_start(out=b2_row[ROW_B2 : ROW_B2 + 1, :], in_=b2.rearrange("(o e) -> o e", o=1))
        w3_pieces = [(g, j) for j in range(HALVES) for g in range(PASSES)]
        for g, j in w3_pieces:
            cols = slice(j * BANK, (j + 1) * BANK)
            w3_raw[g, j] = keep.tile([P, PACK, BANK], BF16, name="w3_raw%d%d" % (g, j))
            nc.sync.dma_start(out=w3_raw[g, j][:], in_=w3_view[:, g, :, cols])
            if (g, j) == w3_pieces[0]:
                nc.sync.dma_start(out=vecs[ROW_B3 : ROW_B3 + 8, :], in_=b3.rearrange("(c p) -> c p", p=P))
                nc.sync.dma_start(out=vecs[ROW_G : ROW_G + 8, :], in_=ln_g.rearrange("(c p) -> c p", p=P))
                nc.sync.dma_start(out=vecs[ROW_MASK : ROW_MASK + 1, :], in_=mask_row)
                nc.sync.dma_start(out=lnb_row[ROW_MASK : ROW_MASK + 1, :], in_=ln_b.rearrange("(o e) -> o e", o=1))

        ident_f32 = keep.tile([P, P], F32)
        ident_bf16 = keep.tile([P, P], BF16)
        make_identity(nc, ident_bf16[:])
        make_identity(nc, ident_f32[:])
        table_warm = keep.tile([P, 1], F32)
        nc.scalar.activation(out=table_warm[:], in_=one[:], func=ACT.Abs_reciprocal_sqrt)

        w2_codes = keep.tile([P, PASSES, E], U32, align_bytes=64)
        w2_scales = keep.tile([P, PASSES, E], U8, align_bytes=64)
        w3_codes = keep.tile([P, PASSES, E], U32, align_bytes=64)
        w3_scales = keep.tile([P, PASSES, E], U8, align_bytes=64)
        h1_codes = keep.tile([P, PASSES * P], U32, align_bytes=64)
        h1_scales = keep.tile([P, PASSES * P], U8, align_bytes=64)
        h_codes = keep.tile([P, PASSES * P], U32, align_bytes=64)
        h_scales = keep.tile([P, PASSES * P], U8, align_bytes=64)

        def regroup(raw, g, j, vector_cols):
            grouped = stage.tile([P, BANK, PACK], BF16, align_bytes=64, name="grouped")
            src = raw[g, j][:].rearrange("p t (c i) -> p c t i", i=RUN)
            if raw is w2_raw:
                dst = grouped[:].rearrange("p (i c) t -> p c t i", i=RUN)
            else:
                dst = grouped[:].rearrange("p (c i) t -> p c t i", i=RUN)
            cut = vector_cols // RUN
            nc.vector.tensor_copy(out=dst[:, :cut], in_=src[:, :cut])
            nc.scalar.copy(out=dst[:, cut:], in_=src[:, cut:])
            return grouped

        def quantise(grouped, codes, scales, g, j):
            cols = slice(j * BANK, (j + 1) * BANK)
            nc.vector.quantize_mx(
                out=codes[:, g, cols].bitcast(FP8X4),
                scales=scales[:, g, cols],
                in_=grouped[:].rearrange("p w t -> p (w t)"),
            )

        hidden_ps = [psum.tile([P, BLOCKS, P], F32, name="hidden%d" % j, tag="hidden%d" % j) for j in range(HALVES)]

        def layer1(j):
            for t in range(BLOCKS):
                units = slice(j * BANK + t * P, j * BANK + (t + 1) * P)
                for g in range(PASSES):
                    tokens = slice(g * P, (g + 1) * P)
                    nc.tensor.matmul_mx(
                        out=hidden_ps[j][:, t, :],
                        lhsT=w2_codes[:, g, units].bitcast(FP8X4),
                        lhsT_scale=w2_scales[:, g, units],
                        rhs=h1_codes[:, tokens].bitcast(FP8X4),
                        rhs_scale=h1_scales[:, tokens],
                        start=(g == 0),
                        stop=(g == PASSES - 1),
                    )

        w2_grouped = [regroup(w2_raw, *pieces[0], FIRST_VECTOR_COLS)]
        quantise(w2_grouped[0], w2_codes, w2_scales, *pieces[0])

        def spread(row, blocks, name, tag):
            rows_ps = psum.tile([P, blocks * P], BF16, name=name, tag=tag)
            for c in range(blocks):
                nc.tensor.transpose(
                    rows_ps[:, c * P : (c + 1) * P],
                    vecs_t[:, row + c : row + c + 1].to_broadcast([P, P]),
                    ident_bf16[:],
                )
            return rows_ps

        h1_words = h1_sb[:].bitcast(F32).rearrange("r (g p u) -> r g u p", g=PASSES, u=2)
        h1_ps = psum.tile([P, PASSES * 2, P], F32, tag="h1_then_y1")
        for g in range(PASSES):
            for u in range(2):
                nc.tensor.transpose(h1_ps[:, 2 * g + u, :], h1_words[:, g, u, :], ident_f32[:])
        h1_grouped = keep.tile([P, PASSES * P * PACK], BF16, align_bytes=64)
        nc.scalar.copy(
            out=h1_grouped[:].bitcast(F32).rearrange("p (g r u) -> p g r u", g=PASSES, u=2),
            in_=h1_ps[:].rearrange("p (g u) r -> p g r u", u=2),
        )

        w2_grouped.append(regroup(w2_raw, *pieces[1], W2_VECTOR_COLS))
        nc.vector.quantize_mx(out=h1_codes[:].bitcast(FP8X4), scales=h1_scales[:], in_=h1_grouped[:])

        b2_ps = psum.tile([P, HALVES * PACK, P], BF16, tag="b2_then_g")
        for j in range(HALVES):
            for t in range(PACK):
                nc.tensor.transpose(
                    b2_ps[:, j * PACK + t, :],
                    b2_row[:, j * BANK + t : (j + 1) * BANK : PACK],
                    ident_bf16[:],
                )
        nc.sync.dma_start(
            out=g_row[ROW_MASK : ROW_MASK + 1, :], in_=ln_g.rearrange("(j o n) -> j o n", j=HALVES, o=1)[0]
        )

        for step in range(2, len(pieces)):
            w2_grouped.append(regroup(w2_raw, *pieces[step], W2_VECTOR_COLS))
            quantise(w2_grouped[step - 1], w2_codes, w2_scales, *pieces[step - 1])
        layer1(0)

        w3_grouped = [regroup(w3_raw, *w3_pieces[0], W3_VECTOR_COLS)]
        b2_cols = keep.tile([P, HALVES * PACK], BF16)
        nc.scalar.copy(out=b2_cols[:], in_=b2_ps[:, :, ROW_B2])
        quantise(w2_grouped[-1], w2_codes, w2_scales, *pieces[-1])
        vecs_ps = psum.tile([P, P], BF16, tag="vecs_then_y0")
        nc.tensor.transpose(vecs_ps[:], vecs[:], ident_bf16[:])
        layer1(1)

        w3_grouped.append(regroup(w3_raw, *w3_pieces[1], W3_VECTOR_COLS))
        quantise(w3_grouped[0], w3_codes, w3_scales, *w3_pieces[0])
        vecs_t = keep.tile([P, ROWS_USED], BF16)
        nc.vector.tensor_copy(out=vecs_t[:], in_=vecs_ps[:, :ROWS_USED])
        mask_col = keep.tile([P, 1], F32)
        nc.gpsimd.tensor_copy(out=mask_col[:], in_=vecs_t[:, ROW_MASK : ROW_MASK + 1])
        b3_ps = spread(ROW_B3, E // P, "b3_ps", "b3")
        shift_ps = []
        for j in range(HALVES):
            shift_j = psum.tile([P, BANK], F32, name="shift%d" % j)
            nc.tensor.matmul(
                shift_j[:], lhsT=vecs[:], rhs=lnb_row[:, j * BANK : (j + 1) * BANK], start=True, stop=True
            )
            shift_ps.append(shift_j)

        biased = keep.tile([P, HALVES, P, PACK], BF16)
        for j in range(HALVES):
            nc.vector.tensor_tensor(
                out=biased[:, j],
                in0=hidden_ps[j][:].rearrange("p t r -> p r t"),
                in1=b2_cols[:, j * PACK : (j + 1) * PACK].unsqueeze(1).to_broadcast([P, P, PACK]),
                op=ALU.add,
            )

        w3_grouped.append(regroup(w3_raw, *w3_pieces[2], W3_VECTOR_COLS))
        h_grouped = keep.tile([P, PASSES * P * PACK], BF16, align_bytes=64)
        nc.vector.tensor_scalar_max(
            out=h_grouped[:], in0=biased[:].rearrange("p j r t -> p (j r t)"), scalar1=0.0
        )
        quantise(w3_grouped[1], w3_codes, w3_scales, *w3_pieces[1])
        nc.vector.quantize_mx(out=h_codes[:].bitcast(FP8X4), scales=h_scales[:], in_=h_grouped[:])

        y_ps = [
            psum.tile([P, BANK], F32, name="y0", tag="vecs_then_y0"),
            psum.tile([P, BANK], F32, name="y1", tag="h1_then_y1"),
        ]

        def layer2(g, j):
            tokens = slice(g * P, (g + 1) * P)
            cols = slice(j * BANK, (j + 1) * BANK)
            nc.tensor.matmul_mx(
                out=y_ps[j][:],
                lhsT=h_codes[:, tokens].bitcast(FP8X4),
                lhsT_scale=h_scales[:, tokens],
                rhs=w3_codes[:, g, cols].bitcast(FP8X4),
                rhs_scale=w3_scales[:, g, cols],
                start=(g == 0),
                stop=(g == PASSES - 1),
            )

        z = keep.tile([P, E], F32)
        first, second = slice(0, BANK), slice(BANK, E)

        layer2(*w3_pieces[0])
        layer2(*w3_pieces[1])
        w3_grouped.append(regroup(w3_raw, *w3_pieces[3], W3_VECTOR_COLS))
        b3_all = keep.tile([P, E], BF16)
        nc.scalar.copy(out=b3_all[:], in_=b3_ps[:])
        quantise(w3_grouped[2], w3_codes, w3_scales, *w3_pieces[2])
        layer2(*w3_pieces[2])
        quantise(w3_grouped[3], w3_codes, w3_scales, *w3_pieces[3])
        layer2(*w3_pieces[3])

        g0_ps = psum.tile([P, BANK], F32, name="g0_ps", tag="hidden0")
        nc.tensor.matmul(g0_ps[:], lhsT=vecs[:], rhs=g_row[:], start=True, stop=True)
        g1_ps = spread(ROW_G + BLOCKS, BLOCKS, "g1_ps", "b2_then_g")

        def add_b3(j, cols, total):
            nc.vector.scalar_tensor_tensor(
                out=z[:, cols],
                in0=y_ps[j][:],
                scalar=1.0,
                in1=b3_all[:, cols],
                op0=ALU.mult,
                op1=ALU.add,
                accum_out=total[:],
            )

        squares = keep.tile([P, E], F32)

        def square(cols, total):
            nc.scalar.activation(
                out=squares[:, cols], in_=z[:, cols], func=ACT.Square, bias=neg_m0[:], accum_out=total[:]
            )

        sum0, sum1 = keep.tile([P, 1], F32, name="sum0"), keep.tile([P, 1], F32, name="sum1")
        sq0, sq1 = keep.tile([P, 1], F32, name="sq0"), keep.tile([P, 1], F32, name="sq1")
        add_b3(0, first, sum0)
        neg_m0 = keep.tile([P, 1], F32)
        nc.scalar.activation(out=neg_m0[:], in_=sum0[:], func=ACT.Copy, scale=-1.0 / BANK)
        half_m0 = keep.tile([P, 1], F32)
        nc.scalar.activation(out=half_m0[:], in_=sum0[:], func=ACT.Copy, scale=1.0 / E)
        square(first, sq0)
        add_b3(1, second, sum1)
        square(second, sq1)

        offset = keep.tile([P, 1], F32)
        nc.gpsimd.tensor_scalar(
            out=offset[:], in0=sum1[:], scalar1=1.0 / E, scalar2=half_m0[:], op0=ALU.mult, op1=ALU.subtract
        )
        var0 = keep.tile([P, 1], F32)
        nc.gpsimd.tensor_scalar(
            out=var0[:], in0=sq0[:], scalar1=1.0 / E, scalar2=EPS, op0=ALU.mult, op1=ALU.add
        )
        neg_var0 = keep.tile([P, 1], F32)
        nc.gpsimd.tensor_scalar(
            out=neg_var0[:], in0=offset[:], scalar1=offset[:], scalar2=var0[:], op0=ALU.mult, op1=ALU.subtract
        )
        rstd = keep.tile([P, 1], F32)
        nc.scalar.activation(
            out=rstd[:], in_=sq1[:], func=ACT.Abs_reciprocal_sqrt, scale=-1.0 / E, bias=neg_var0[:]
        )
        rstd_mask = keep.tile([P, 1], F32)
        nc.scalar.activation(out=rstd_mask[:], in_=rstd[:], func=ACT.Copy, scale=mask_col[:])
        mean = keep.tile([P, 1], F32)
        nc.vector.tensor_scalar(
            out=mean[:], in0=sum1[:], scalar1=1.0 / E, scalar2=half_m0[:], op0=ALU.mult, op1=ALU.add
        )
        centred = keep.tile([P, E], F32)
        for cols, gain in ((first, g0_ps), (second, g1_ps)):
            nc.vector.scalar_tensor_tensor(
                out=centred[:, cols], in0=z[:, cols], scalar=mean[:], in1=gain[:], op0=ALU.subtract, op1=ALU.mult
            )
        result = keep.tile([P, E], F32)
        for j in range(HALVES):
            for lo, hi in ((0, STORE_CUTS[j]), (STORE_CUTS[j], BANK)):
                in_bank = slice(lo, hi)
                cols = slice(j * BANK + lo, j * BANK + hi)
                nc.vector.scalar_tensor_tensor(
                    out=result[:, cols],
                    in0=centred[:, cols],
                    scalar=(rstd if j == 0 else rstd_mask)[:],
                    in1=shift_ps[j][:, in_bank],
                    op0=ALU.mult,
                    op1=ALU.add,
                )
                nc.sync.dma_start(out=out_rows[:, cols], in_=result[:, cols])
